import numpy as np
import ml_dtypes


def mxq(x, axis, fmt="e4m3"):
    dtype, down = {"e4m3": (ml_dtypes.float8_e4m3fn, 7), "e5m2": (ml_dtypes.float8_e5m2, 14)}[fmt]
    v = np.moveaxis(np.asarray(x, np.float32).astype(ml_dtypes.bfloat16).astype(np.float64), axis, -1)
    blocks = v.reshape(v.shape[:-1] + (-1, 32))
    amax = np.abs(blocks).max(-1, keepdims=True)
    byte = np.maximum(np.where(amax > 0, np.frexp(amax)[1] - 1 + 127, 0) - down, 1)
    scale = np.exp2(byte - 127.0)
    codes = (blocks / scale).astype(np.float32).astype(dtype).astype(np.float64)
    return np.moveaxis((codes * scale).reshape(v.shape), -1, axis)


WIDE = False


def mx_kscale(k):
    if not WIDE:
        return np.ones(k)
    levels = np.array([10, -10, 5, -5, 0])
    if k % 512:
        return np.exp2(np.random.permutation(np.resize(levels, k // 32))).repeat(32)
    a = np.empty((k // 512, 16))
    for p in range(k // 512):
        a[p, :8] = np.random.permutation(np.resize(levels, 8))
        for g in range(8):
            far = levels[np.abs(levels - a[p, g]) >= 10]
            a[p, g + 8] = far[np.random.randint(len(far))]
    return np.exp2(a.ravel()).repeat(32)


BF16 = ml_dtypes.bfloat16


def bf(x):
    return np.asarray(x, np.float32).astype(BF16)


def f64(x):
    return np.asarray(x).astype(np.float64)


B, S, E, H, C = 1, 512, 2048, 16, 512
HD = E // H
EPS = 1e-5


def silu(v):
    return v / (1.0 + np.exp(-v))


def draw0():
    s, t = mx_kscale(E), mx_kscale(E)
    spread = np.exp(0.7 * np.random.standard_normal((B, S, H, 1)))
    shift = 0.5 * np.random.standard_normal((B, S, H, 1))
    attn = 1.5 * (np.random.standard_normal((B, S, H, HD)) * spread + shift)
    return {"x": bf(np.random.standard_normal((B, S, E)) * s),
            "attn": bf(attn.reshape(B, S, E)),
            "Wg": bf(np.random.standard_normal((E, E)) / np.sqrt(E) / s[:, None]),
            "bg": bf(np.random.standard_normal(E) * 0.2),
            "gn_w": bf((1.0 + 0.1 * np.random.standard_normal(E)) * t),
            "gn_b": bf(0.1 * np.random.standard_normal(E) * t),
            "Wo": bf(np.random.standard_normal((E, E)) * 1.5 / np.sqrt(E) / t[:, None]),
            "bo": bf(np.random.standard_normal(E) * 0.1)}


def core(x, attn, Wg, bg, gn_w, gn_b, Wo, bo):
    g = f64(attn).reshape(B, S, H, HD)
    mu = g.mean(-1, keepdims=True)
    var = g.var(-1, keepdims=True)
    g = (g - mu) / np.sqrt(var + EPS)
    g = g.reshape(B, S, E) * f64(gn_w) + f64(gn_b)
    gate = silu((mxq(f64(x), 2, "e4m3") @ mxq(f64(Wg), 0, "e4m3")) + f64(bg))
    h = gate * g
    return (mxq(h, 2, "e4m3") @ mxq(f64(Wo), 0, "e4m3")) + f64(bo)


def e4m3fn_bytes(y):
    return np.clip(np.asarray(y, np.float64), -448.0, 448.0).astype(np.float32).astype(ml_dtypes.float8_e4m3fn).view(np.uint8)


def e4m3fn_values(b):
    return np.asarray(b, np.uint8).view(ml_dtypes.float8_e4m3fn).astype(np.float64)


def setup_inputs():
    d = draw0()
    x0 = np.asarray(d['Wo']).astype(np.float64)
    s = (np.max(np.abs(x0), axis=(1,), keepdims=True) / 448.0).astype(np.float32)
    out = {}
    for k, v in d.items():
        if k == 'Wo':
            out['Wo_bytes'] = e4m3fn_bytes(x0 / s.astype(np.float64))
            out['Wo_scale'] = s
        else:
            out[k] = v
    return out


def reference(x, attn, Wg, bg, gn_w, gn_b, Wo_bytes, Wo_scale, bo):
    return core(x, attn, Wg, bg, gn_w, gn_b, e4m3fn_values(Wo_bytes) * Wo_scale.astype(np.float64), bo)

@@ -1,0 +1,390 @@
+from contextlib import ExitStack
+
+import concourse.mybir as mybir
+from concourse.masks import make_identity
+
+TOK, E = 512, 2048
+HD = 128
+EPS = 1e-5
+FLOPS = 2 * (2 * TOK * E * E)
+
+P = 128
+T = 4
+KP = P * T
+NP = E // KP
+NI = TOK // P
+
+F32 = mybir.dt.float32
+BF16 = mybir.dt.bfloat16
+U32 = mybir.dt.uint32
+U8 = mybir.dt.uint8
+FP8 = mybir.dt.float8_e4m3fn
+FP8X4 = mybir.dt.float8_e4m3fn_x4
+ALU = mybir.AluOpType
+ACT = mybir.ActivationFunctionType
+
+IL_W = ("SPSV", "VVSV", "VVSV", "VVVV")
+IL_O_SCALAR = ()
+
+
+def tile_multiscaleretention_pb_kernel(
+    tc, x, attn, Wg, bg, gn_w, gn_b, Wo_bytes, Wo_scale, bo, out
+):
+    nc = tc.nc
+    x2 = x.rearrange("o s e -> (o s) e")
+    a2 = attn.rearrange("o s e -> (o s) e")
+    out2 = out.rearrange("o s e -> (o s) e")
+    wg4 = Wg.rearrange("(c p j) n -> c p j n", p=P, j=T)
+    wo4 = Wo_bytes.rearrange("(g p t) n -> g p t n", p=P, t=T)
+
+    with ExitStack() as ctx:
+        keep = ctx.enter_context(tc.tile_pool(name="keep", bufs=1))
+        rot = ctx.enter_context(tc.tile_pool(name="rot", bufs=2))
+        psum = ctx.enter_context(tc.psum_pool(name="psum", bufs=8))
+        ctx.enter_context(tc.manual_schedule())
+
+        def bank(name):
+            return psum.tile([P, 512], F32, tag="bank", name=name, bufs=8)
+
+        def il_tile(name, tag="il", bufs=6):
+            return rot.tile([P, T * 512], BF16, tag=tag, name=name, bufs=bufs, align_bytes=64)
+
+        at, xs, wraw = [], [], {}
+
+        def load_attn(i):
+            a = keep.tile([P, E], BF16, name="at%d" % i, align_bytes=64)
+            pieces = 2 if i == 0 else 1
+            for k in range(pieces):
+                cols = slice(k * E // pieces, (k + 1) * E // pieces)
+                nc.sync.dma_start(out=a[:, cols], in_=a2[i * P : (i + 1) * P, cols])
+            at.append(a)
+
+        def load_x(i):
+            a = rot.tile([P, E], BF16, tag="in4k", name="xs%d" % i, bufs=8, align_bytes=64)
+            nc.sync.dma_start(out=a[:], in_=x2[i * P : (i + 1) * P, :])
+            xs.append(a)
+
+        def load_w(g, c):
+            a = rot.tile([P, T, 512], BF16, tag="in4k", name="w%d%d" % (g, c), bufs=8, align_bytes=64)
+            nc.sync.dma_start(out=a[:], in_=wg4[c][:, :, g * 512 : (g + 1) * 512])
+            wraw[g, c] = a
+
+        vecs16 = keep.tile([P, 3, NP, T], BF16, name="vecs16")
+        wsc = keep.tile([P, NP, T], F32, name="wsc")
+        for v, vec in enumerate((bg, gn_w, gn_b)):
+            nc.scalar.dma_start(out=vecs16[:, v, :, :], in_=vec.rearrange("(g p t) -> p g t", p=P, t=T))
+        nc.scalar.dma_start(out=wsc[:], in_=Wo_scale.rearrange("(g p t) o -> p g (t o)", p=P, t=T))
+
+        for i in range(NI):
+            load_attn(i)
+            load_w(0, i)
+        for i in range(NI):
+            load_x(i)
+
+        warm = keep.tile([P, 1], F32, name="warm")
+        nc.vector.memset(warm[:], 0.0)
+        nc.scalar.activation(out=warm[:], in_=warm[:], func=ACT.Silu)
+        ident = keep.tile([P, P], F32, name="ident")
+        make_identity(nc, ident[:])
+        mhalf = keep.tile([P, 16], F32, name="mhalf")
+        nc.gpsimd.memset(mhalf[:], -0.5)
+        vecs = keep.tile([P, 3, NP, T], F32, name="vecs")
+
+        def col(v, g, t):
+            return vecs[:, v, g, t : t + 1]
+
+        stats = [keep.tile([P, 16, 6], F32, name="st%d" % i) for i in range(NI)]
+        tmp = [keep.tile([P, 4, 16], F32, name="tmp%d" % i) for i in range(NI)]
+        rstd = [keep.tile([P, 16], F32, name="rstd%d" % i) for i in range(NI)]
+        nbias = [keep.tile([P, 16], F32, name="nbias%d" % i) for i in range(NI)]
+
+        def group_stats(i):
+            for q in range(16):
+                nc.vector.bn_stats(out=stats[i][:, q, :], in_=at[i][:, q * HD : (q + 1) * HD])
+
+        def group_combine(i):
+            e = nc.gpsimd
+            s, m = stats[i], tmp[i]
+            e.tensor_tensor(out=m[:, 0, :], in0=s[:, :, 1], in1=s[:, :, 4], op=ALU.add)
+            e.tensor_tensor(out=m[:, 1, :], in0=s[:, :, 1], in1=s[:, :, 4], op=ALU.subtract)
+            e.tensor_tensor(out=m[:, 2, :], in0=s[:, :, 2], in1=s[:, :, 5], op=ALU.add)
+            e.tensor_tensor(out=m[:, 3, :], in0=m[:, 1, :], in1=m[:, 1, :], op=ALU.mult)
+            e.tensor_scalar(out=m[:, 2, :], in0=m[:, 2, :], scalar1=1.0 / HD, scalar2=EPS, op0=ALU.mult, op1=ALU.add)
+            e.tensor_scalar(out=m[:, 3, :], in0=m[:, 3, :], scalar1=0.25, scalar2=0.0, op0=ALU.mult, op1=ALU.add)
+            e.tensor_tensor(out=m[:, 2, :], in0=m[:, 2, :], in1=m[:, 3, :], op=ALU.add)
+            e.tensor_tensor(out=rstd[i][:], in0=m[:, 2, :], in1=mhalf[:], op=ALU.pow)
+            e.tensor_scalar(out=m[:, 0, :], in0=m[:, 0, :], scalar1=-0.5, scalar2=0.0, op0=ALU.mult, op1=ALU.add)
+            e.tensor_tensor(out=nbias[i][:], in0=m[:, 0, :], in1=rstd[i][:], op=ALU.mult)
+
+        nrm = {}
+
+        def normalise(i, g):
+            n = rot.tile([P, T, P], F32, tag="nrm", name="nrm%d%d" % (i, g), bufs=8, align_bytes=64)
+            nrm[i, g] = n
+            for u in range(4):
+                q = 4 * g + u
+                nc.scalar.activation(
+                    out=n[:, :, 32 * u : 32 * (u + 1)],
+                    in_=at[i][:, q * HD : (q + 1) * HD].rearrange("p (m t) -> p t m", t=T),
+                    func=ACT.Identity,
+                    scale=rstd[i][:, q : q + 1],
+                    bias=nbias[i][:, q : q + 1],
+                )
+
+        nbank = {}
+
+        def transpose_norm(g):
+            for t in range(T):
+                b = bank("nT%d%d" % (g, t))
+                nbank[g, t] = b
+                for i in range(NI):
+                    nc.tensor.transpose(b[:, i * P : (i + 1) * P], nrm[i, g][:, t, :], ident[:])
+
+        xbank, xil, xq, xqs = {}, {}, {}, {}
+
+        def transpose_x(c, h):
+            b = bank("xT%d%d" % (c, h))
+            xbank[c, h] = b
+            bv = b[:].rearrange("p (u r) -> p u r", u=2)
+            for i in range(2):
+                words = xs[2 * h + i][:].bitcast(F32)
+                for u in range(2):
+                    nc.tensor.transpose(
+                        bv[:, u, i * P : (i + 1) * P], words[:, 256 * c + u : 256 * (c + 1) : 2], ident[:]
+                    )
+
+        def copy_x(c, h):
+            if h == 0:
+                xil[c] = il_tile("xil%d" % c)
+            copy = nc.vector.tensor_copy if h == 0 else nc.scalar.copy
+            copy(
+                out=xil[c][:].bitcast(F32)[:, 512 * h : 512 * (h + 1)].rearrange("p (r u) -> p r u", u=2),
+                in_=xbank[c, h][:].rearrange("p (u r) -> p r u", u=2),
+            )
+
+        def quant(src, name, codes_pool, tag, bufs):
+            codes = codes_pool.tile([P, 512], U32, tag=tag + "c", name=name + "c", bufs=bufs, align_bytes=64)
+            scales = codes_pool.tile([P, 512], U8, tag=tag + "s", name=name + "s", bufs=bufs, align_bytes=64)
+            nc.vector.quantize_mx(out=codes[:].bitcast(FP8X4), scales=scales[:], in_=src[:])
+            return codes, scales
+
+        wil, wq = {}, {}
+
+        def interleave_w(g, c):
+            eng = IL_W[g][c]
+            d = il_tile("wil%d%d" % (g, c), "ils", 2) if eng == "S" else il_tile("wil%d%d" % (g, c))
+            wil[g, c] = d
+            o = d[:].rearrange("p (t m j) -> p t m j", t=T, j=T)
+            s = wraw[g, c][:].rearrange("p j (m t) -> p t m j", t=T)
+            if eng == "V":
+                nc.vector.tensor_copy(out=o, in_=s)
+            elif eng == "S":
+                nc.scalar.copy(out=o, in_=s)
+
+        def interleave_w_quarter(g, c, t):
+            o = wil[g, c][:].rearrange("p (t m j) -> p t m j", t=T, j=T)
+            s = wraw[g, c][:].rearrange("p j (m t) -> p t m j", t=T)
+            nc.gpsimd.tensor_scalar(
+                out=o[:, t, :, :], in0=s[:, t, :, :], scalar1=1.0, scalar2=0.0, op0=ALU.mult, op1=ALU.add
+            )
+
+        def quant_w(g, c):
+            wq[g, c] = quant(wil[g, c], "wq%d%d" % (g, c), rot, "wq", 8)
+
+        acc, fT, gate, hq = {}, {}, {}, {}
+
+        def gemm1(g):
+            for t in range(T):
+                b = bank("acc%d%d" % (g, t))
+                acc[g, t] = b
+                for c in range(NP):
+                    codes, scales = wq[g, c]
+                    nc.tensor.matmul_mx(
+                        out=b[:],
+                        lhsT=codes[:, t * P : (t + 1) * P].bitcast(FP8X4),
+                        lhsT_scale=scales[:, t * P : (t + 1) * P],
+                        rhs=xq[c][0][:].bitcast(FP8X4),
+                        rhs_scale=xq[c][1][:],
+                        start=(c == 0),
+                        stop=(c == NP - 1),
+                    )
+
+        def gain(g):
+            f = rot.tile([P, T, TOK], F32, tag="f", name="f%d" % g, bufs=2, align_bytes=64)
+            fT[g] = f
+            for t in range(T):
+                nc.scalar.activation(
+                    out=f[:, t, :], in_=nbank[g, t][:], func=ACT.Identity, scale=col(1, g, t), bias=col(2, g, t)
+                )
+
+        def silu(g):
+            f = rot.tile([P, T, TOK], F32, tag="gate", name="gate%d" % g, bufs=2, align_bytes=64)
+            gate[g] = f
+            for t in range(T):
+                nc.scalar.activation(out=f[:, t, :], in_=acc[g, t][:], func=ACT.Silu, bias=col(0, g, t))
+
+        hil = {}
+
+        def product(g):
+            d = il_tile("hil%d" % g)
+            hil[g] = d
+            nc.vector.tensor_tensor(
+                out=d[:].rearrange("p (c i t) -> p c t i", i=4, t=T),
+                in0=fT[g][:].rearrange("p t (c i) -> p c t i", i=4),
+                in1=gate[g][:].rearrange("p t (c i) -> p c t i", i=4),
+                op=ALU.mult,
+            )
+
+        def quant_h(g):
+            hq[g] = quant(hil[g], "hq%d" % g, keep, "hq%d" % g, 1)
+
+        wob, wide, oil, oq = {}, {}, {}, {}
+
+        def load_wo(h, g):
+            b = rot.tile([P, T, 1024], U8, tag="wob", name="wob%d%d" % (h, g), bufs=4, align_bytes=64)
+            nc.sync.dma_start(out=b[:], in_=wo4[g][:, :, h * 1024 : (h + 1) * 1024])
+            wob[h, g] = b
+
+        def widen(n, g):
+            w = rot.tile([P, T, 512], BF16, tag="wide", name="wide%d%d" % (n, g), bufs=4, align_bytes=64)
+            wide[n, g] = w
+            lo = (n % 2) * 512
+            for t in range(T):
+                nc.scalar.activation(
+                    out=w[:, t, :],
+                    in_=wob[n // 2, g][:, t, lo : lo + 512].bitcast(FP8),
+                    func=ACT.Copy,
+                    scale=wsc[:, g, t : t + 1],
+                )
+
+        def interleave_o(n, g):
+            on_scalar = 4 * n + g in IL_O_SCALAR
+            d = il_tile("oil%d%d" % (n, g), "ils", 2) if on_scalar else il_tile("oil%d%d" % (n, g))
+            oil[n, g] = d
+            copy = nc.scalar.copy if on_scalar else nc.vector.tensor_copy
+            copy(out=d[:].rearrange("p (n t) -> p n t", t=T), in_=wide[n, g][:].rearrange("p t n -> p n t"))
+
+        def quant_o(n, g):
+            oq[n, g] = quant(oil[n, g], "oq%d%d" % (n, g), rot, "oq", 8)
+
+        acc2 = {}
+
+        def gemm2(n):
+            for i in range(NI):
+                acc2[n, i] = bank("out%d%d" % (n, i))
+            for g in range(NP):
+                hc, hs = hq[g]
+                codes, scales = oq[n, g]
+                for i in range(NI):
+                    nc.tensor.matmul_mx(
+                        out=acc2[n, i][:],
+                        lhsT=hc[:, i * P : (i + 1) * P].bitcast(FP8X4),
+                        lhsT_scale=hs[:, i * P : (i + 1) * P],
+                        rhs=codes[:].bitcast(FP8X4),
+                        rhs_scale=scales[:],
+                        start=(g == 0),
+                        stop=(g == NP - 1),
+                    )
+
+        bo_sb = keep.tile([P, E], BF16, name="bo_sb")
+
+        def store(n):
+            for i in range(NI):
+                o = rot.tile([P, 512], F32, tag="o", name="o%d%d" % (n, i), bufs=4, align_bytes=64)
+                cols = slice(n * 512, (n + 1) * 512)
+                nc.vector.tensor_tensor(out=o[:], in0=acc2[n, i][:], in1=bo_sb[:, cols], op=ALU.add)
+                nc.sync.dma_start(out=out2[i * P : (i + 1) * P, cols], in_=o[:])
+
+        interleave_w(0, 0)
+        interleave_w(0, 1)
+        load_w(1, 0)
+        group_stats(0)
+        group_combine(0)
+        normalise(0, 0)
+        normalise(0, 1)
+        group_stats(1)
+        for t in range(2):
+            interleave_w_quarter(0, 1, t)
+        group_combine(1)
+        interleave_w(0, 2)
+        normalise(1, 0)
+        normalise(1, 1)
+        group_stats(2)
+        for t in range(2, 4):
+            interleave_w_quarter(0, 1, t)
+        load_w(1, 1)
+        load_w(1, 2)
+        group_combine(2)
+        normalise(2, 0)
+        normalise(2, 1)
+        group_stats(3)
+        group_combine(3)
+        nc.gpsimd.tensor_copy(out=vecs[:], in_=vecs16[:])
+        for c in range(3):
+            quant_w(0, c)
+        for c in range(NP):
+            transpose_x(c, 0)
+            copy_x(c, 0)
+        interleave_w(0, 3)
+        load_w(1, 3)
+        normalise(3, 0)
+        for c in range(NP):
+            transpose_x(c, 1)
+            copy_x(c, 1)
+        transpose_norm(0)
+        quant_w(0, 3)
+        for c in range(NP):
+            xq[c] = quant(xil[c], "xq%d" % c, keep, "xq%d" % c, 1)
+        for k in range(4):
+            load_w(2, k)
+        normalise(3, 1)
+        gain(0)
+        interleave_w(1, 2)
+
+        for g in range(NP):
+            gemm1(g)
+            if g + 1 < NP:
+                for c in range(NP):
+                    if IL_W[g + 1][c] == "V":
+                        interleave_w(g + 1, c)
+                for c in range(NP):
+                    quant_w(g + 1, c)
+                if g < 1:
+                    for k in range(4):
+                        load_w(3, k)
+                if g == 1:
+                    for k in range(NP):
+                        load_wo(0, k)
+                    nc.sync.dma_start(out=bo_sb[:], in_=bo.partition_broadcast(P))
+            silu(g)
+            if g + 1 < NP:
+                transpose_norm(g + 1)
+                gain(g + 1)
+            if g + 2 < NP:
+                for c in range(NP):
+                    if IL_W[g + 2][c] == "S":
+                        interleave_w(g + 2, c)
+                for i in range(NI):
+                    normalise(i, g + 2)
+            if g == NP - 2:
+                widen(0, 0)
+                widen(0, 1)
+            if g == NP - 1:
+                interleave_o(0, 0)
+                interleave_o(0, 1)
+            product(g)
+            quant_h(g)
+
+        units = [(n, g) for n in range(4) for g in range(NP)]
+        for k, (n, g) in enumerate(units):
+            if k + 2 < len(units):
+                widen(*units[k + 2])
+                if 4 <= k + 2 < 8:
+                    load_wo(1, k - 2)
+                interleave_o(*units[k + 2])
+            quant_o(n, g)
+            if g == NP - 1:
+                gemm2(n)
+            if g == 1 and n > 0:
+                store(n - 1)
+        store(3)

@@ -24,7 +24,7 @@ ALU = mybir.AluOpType
 ACT = mybir.ActivationFunctionType
 
 IL_W = ("SPSV", "VVSV", "VVSV", "VVVV")
-IL_O_SCALAR = ()
+IL_O = "VVVVVVVVVVVVVVVV"
 
 
 def tile_multiscaleretention_pb_kernel(
@@ -86,6 +86,8 @@ def tile_multiscaleretention_pb_kernel(
         nc.scalar.activation(out=warm[:], in_=warm[:], func=ACT.Silu)
         ident = keep.tile([P, P], F32, name="ident")
         make_identity(nc, ident[:])
+        identb = keep.tile([P, P], BF16, name="identb")
+        nc.gpsimd.tensor_copy(out=identb[:], in_=ident[:])
         mhalf = keep.tile([P, 16], F32, name="mhalf")
         nc.gpsimd.memset(mhalf[:], -0.5)
         vecs = keep.tile([P, 3, NP, T], F32, name="vecs")
@@ -124,8 +126,8 @@ def tile_multiscaleretention_pb_kernel(
             for u in range(4):
                 q = 4 * g + u
                 nc.scalar.activation(
-                    out=n[:, :, 32 * u : 32 * (u + 1)],
-                    in_=at[i][:, q * HD : (q + 1) * HD].rearrange("p (m t) -> p t m", t=T),
+                    out=n[:, :, 32 * u : 32 * (u + 1)].rearrange("p t m -> p m t"),
+                    in_=at[i][:, q * HD : (q + 1) * HD].rearrange("p (m t) -> p m t", t=T),
                     func=ACT.Identity,
                     scale=rstd[i][:, q : q + 1],
                     bias=nbias[i][:, q : q + 1],
@@ -168,24 +170,37 @@ def tile_multiscaleretention_pb_kernel(
             nc.vector.quantize_mx(out=codes[:].bitcast(FP8X4), scales=scales[:], in_=src[:])
             return codes, scales
 
+        def tensor_interleave(d, sources, name, eng):
+            for half in range(2):
+                b = psum.tile([P, 1024], BF16, tag="bank", name=name + "ab"[half], bufs=8)
+                for k in range(2):
+                    nc.tensor.matmul(
+                        b[:, 512 * k : 512 * (k + 1)], lhsT=identb[:], rhs=sources[2 * half + k], start=True, stop=True
+                    )
+                copy = nc.scalar.copy if eng == "T" else nc.vector.tensor_copy
+                copy(out=d[:, 1024 * half : 1024 * (half + 1)], in_=b[:])
+
         wil, wq = {}, {}
 
         def interleave_w(g, c):
             eng = IL_W[g][c]
-            d = il_tile("wil%d%d" % (g, c), "ils", 2) if eng == "S" else il_tile("wil%d%d" % (g, c))
+            d = il_tile("wil%d%d" % (g, c), "ils", 2) if eng in "ST" else il_tile("wil%d%d" % (g, c))
             wil[g, c] = d
-            o = d[:].rearrange("p (t m j) -> p t m j", t=T, j=T)
-            s = wraw[g, c][:].rearrange("p j (m t) -> p t m j", t=T)
-            if eng == "V":
+            o = d[:].rearrange("p (t m j) -> p m t j", t=T, j=T)
+            s = wraw[g, c][:].rearrange("p j (m t) -> p m t j", t=T)
+            if eng in "TU":
+                tensor_interleave(d, [s[:, :, t, :] for t in range(T)], "pw%d%d" % (g, c), eng)
+            elif eng == "V":
                 nc.vector.tensor_copy(out=o, in_=s)
             elif eng == "S":
                 nc.scalar.copy(out=o, in_=s)
 
-        def interleave_w_quarter(g, c, t):
-            o = wil[g, c][:].rearrange("p (t m j) -> p t m j", t=T, j=T)
-            s = wraw[g, c][:].rearrange("p j (m t) -> p t m j", t=T)
+        def interleave_w_quarter(g, c, k):
+            o = wil[g, c][:].rearrange("p (t m j) -> p m t j", t=T, j=T)
+            s = wraw[g, c][:].rearrange("p j (m t) -> p m t j", t=T)
+            m = slice(32 * k, 32 * (k + 1))
             nc.gpsimd.tensor_scalar(
-                out=o[:, t, :, :], in0=s[:, t, :, :], scalar1=1.0, scalar2=0.0, op0=ALU.mult, op1=ALU.add
+                out=o[:, m, :, :], in0=s[:, m, :, :], scalar1=1.0, scalar2=0.0, op0=ALU.mult, op1=ALU.add
             )
 
         def quant_w(g, c):
@@ -258,11 +273,15 @@ def tile_multiscaleretention_pb_kernel(
                 )
 
         def interleave_o(n, g):
-            on_scalar = 4 * n + g in IL_O_SCALAR
-            d = il_tile("oil%d%d" % (n, g), "ils", 2) if on_scalar else il_tile("oil%d%d" % (n, g))
+            eng = IL_O[4 * n + g]
+            d = il_tile("oil%d%d" % (n, g), "ils", 2) if eng in "ST" else il_tile("oil%d%d" % (n, g))
             oil[n, g] = d
-            copy = nc.scalar.copy if on_scalar else nc.vector.tensor_copy
-            copy(out=d[:].rearrange("p (n t) -> p n t", t=T), in_=wide[n, g][:].rearrange("p t n -> p n t"))
+            s = wide[n, g][:].rearrange("p t n -> p n t")
+            if eng in "TU":
+                tensor_interleave(d, [s[:, k * P : (k + 1) * P] for k in range(4)], "po%d%d" % (n, g), eng)
+            else:
+                copy = nc.scalar.copy if eng == "S" else nc.vector.tensor_copy
+                copy(out=d[:].rearrange("p (n t) -> p n t", t=T), in_=s)
 
         def quant_o(n, g):
             oq[n, g] = quant(oil[n, g], "oq%d%d" % (n, g), rot, "oq", 8)
@@ -320,11 +339,11 @@ def tile_multiscaleretention_pb_kernel(
         group_stats(3)
         group_combine(3)
         nc.gpsimd.tensor_copy(out=vecs[:], in_=vecs16[:])
-        for c in range(3):
-            quant_w(0, c)
         for c in range(NP):
             transpose_x(c, 0)
             copy_x(c, 0)
+        for c in range(3):
+            quant_w(0, c)
         interleave_w(0, 3)
         load_w(1, 3)
         normalise(3, 0)

@@ -88,35 +88,53 @@ def tile_multiscaleretention_pb_kernel(
         make_identity(nc, ident[:])
         identb = keep.tile([P, P], BF16, name="identb")
         nc.gpsimd.tensor_copy(out=identb[:], in_=ident[:])
-        mhalf = keep.tile([P, 16], F32, name="mhalf")
+        mhalf = keep.tile([P, 2, 16], F32, name="mhalf")
         nc.gpsimd.memset(mhalf[:], -0.5)
         vecs = keep.tile([P, 3, NP, T], F32, name="vecs")
 
         def col(v, g, t):
             return vecs[:, v, g, t : t + 1]
 
-        stats = [keep.tile([P, 16, 6], F32, name="st%d" % i) for i in range(NI)]
-        tmp = [keep.tile([P, 4, 16], F32, name="tmp%d" % i) for i in range(NI)]
-        rstd = [keep.tile([P, 16], F32, name="rstd%d" % i) for i in range(NI)]
-        nbias = [keep.tile([P, 16], F32, name="nbias%d" % i) for i in range(NI)]
+        stats = keep.tile([P, NI, 16, 6], F32, name="stats")
+        msum = keep.tile([P, NI, 16], F32, name="msum")
+        mdif = keep.tile([P, NI, 16], F32, name="mdif")
+        var = keep.tile([P, NI, 16], F32, name="var")
+        rstd = keep.tile([P, NI, 16], F32, name="rstd")
+        nbias = keep.tile([P, NI, 16], F32, name="nbias")
 
-        def group_stats(i):
-            for q in range(16):
-                nc.vector.bn_stats(out=stats[i][:, q, :], in_=at[i][:, q * HD : (q + 1) * HD])
+        def group_stats(i, lo, hi):
+            for q in range(lo, hi):
+                nc.vector.bn_stats(out=stats[:, i, q, :], in_=at[i][:, q * HD : (q + 1) * HD])
 
-        def group_combine(i):
-            e = nc.gpsimd
-            s, m = stats[i], tmp[i]
-            e.tensor_tensor(out=m[:, 0, :], in0=s[:, :, 1], in1=s[:, :, 4], op=ALU.add)
-            e.tensor_tensor(out=m[:, 1, :], in0=s[:, :, 1], in1=s[:, :, 4], op=ALU.subtract)
-            e.tensor_tensor(out=m[:, 2, :], in0=s[:, :, 2], in1=s[:, :, 5], op=ALU.add)
-            e.tensor_tensor(out=m[:, 3, :], in0=m[:, 1, :], in1=m[:, 1, :], op=ALU.mult)
-            e.tensor_scalar(out=m[:, 2, :], in0=m[:, 2, :], scalar1=1.0 / HD, scalar2=EPS, op0=ALU.mult, op1=ALU.add)
-            e.tensor_scalar(out=m[:, 3, :], in0=m[:, 3, :], scalar1=0.25, scalar2=0.0, op0=ALU.mult, op1=ALU.add)
-            e.tensor_tensor(out=m[:, 2, :], in0=m[:, 2, :], in1=m[:, 3, :], op=ALU.add)
-            e.tensor_tensor(out=rstd[i][:], in0=m[:, 2, :], in1=mhalf[:], op=ALU.pow)
-            e.tensor_scalar(out=m[:, 0, :], in0=m[:, 0, :], scalar1=-0.5, scalar2=0.0, op0=ALU.mult, op1=ALU.add)
-            e.tensor_tensor(out=nbias[i][:], in0=m[:, 0, :], in1=rstd[i][:], op=ALU.mult)
+        def combine_a(b):
+            e, s = nc.vector, stats[:, 2 * b : 2 * b + 2]
+            k = slice(2 * b, 2 * b + 2)
+            e.tensor_tensor(out=mdif[:, k], in0=s[:, :, :, 1], in1=s[:, :, :, 4], op=ALU.subtract)
+            e.scalar_tensor_tensor(
+                out=var[:, k], in0=s[:, :, :, 2], scalar=HD * EPS, in1=s[:, :, :, 5], op0=ALU.add, op1=ALU.add
+            )
+            e.tensor_tensor(out=msum[:, k], in0=s[:, :, :, 1], in1=s[:, :, :, 4], op=ALU.add)
+
+        def combine_b(b):
+            e = nc.vector
+            k = slice(2 * b, 2 * b + 2)
+            e.scalar_tensor_tensor(
+                out=mdif[:, k], in0=mdif[:, k], scalar=0.25, in1=mdif[:, k], op0=ALU.mult, op1=ALU.mult
+            )
+
+        def combine_c(b):
+            e = nc.vector
+            k = slice(2 * b, 2 * b + 2)
+            e.scalar_tensor_tensor(
+                out=var[:, k], in0=var[:, k], scalar=1.0 / HD, in1=mdif[:, k], op0=ALU.mult, op1=ALU.add
+            )
+            nc.gpsimd.tensor_tensor(out=rstd[:, k], in0=var[:, k], in1=mhalf[:], op=ALU.pow)
+
+        def combine_d(b):
+            k = slice(2 * b, 2 * b + 2)
+            nc.vector.scalar_tensor_tensor(
+                out=nbias[:, k], in0=msum[:, k], scalar=-0.5, in1=rstd[:, k], op0=ALU.mult, op1=ALU.mult
+            )
 
         nrm = {}
 
@@ -129,8 +147,8 @@ def tile_multiscaleretention_pb_kernel(
                     out=n[:, :, 32 * u : 32 * (u + 1)].rearrange("p t m -> p m t"),
                     in_=at[i][:, q * HD : (q + 1) * HD].rearrange("p (m t) -> p m t", t=T),
                     func=ACT.Identity,
-                    scale=rstd[i][:, q : q + 1],
-                    bias=nbias[i][:, q : q + 1],
+                    scale=rstd[:, i, q : q + 1],
+                    bias=nbias[:, i, q : q + 1],
                 )
 
         nbank = {}
@@ -186,10 +204,11 @@ def tile_multiscaleretention_pb_kernel(
             eng = IL_W[g][c]
             d = il_tile("wil%d%d" % (g, c), "ils", 2) if eng in "ST" else il_tile("wil%d%d" % (g, c))
             wil[g, c] = d
-            o = d[:].rearrange("p (t m j) -> p m t j", t=T, j=T)
-            s = wraw[g, c][:].rearrange("p j (m t) -> p m t j", t=T)
+            o = d[:].rearrange("p (t m j) -> p m j t", t=T, j=T)
+            s = wraw[g, c][:].rearrange("p j (m t) -> p m j t", t=T)
             if eng in "TU":
-                tensor_interleave(d, [s[:, :, t, :] for t in range(T)], "pw%d%d" % (g, c), eng)
+                s = wraw[g, c][:].rearrange("p j (m t) -> p t m j", t=T)
+                tensor_interleave(d, [s[:, t] for t in range(T)], "pw%d%d" % (g, c), eng)
             elif eng == "V":
                 nc.vector.tensor_copy(out=o, in_=s)
             elif eng == "S":
@@ -281,7 +300,10 @@ def tile_multiscaleretention_pb_kernel(
                 tensor_interleave(d, [s[:, k * P : (k + 1) * P] for k in range(4)], "po%d%d" % (n, g), eng)
             else:
                 copy = nc.scalar.copy if eng == "S" else nc.vector.tensor_copy
-                copy(out=d[:].rearrange("p (n t) -> p n t", t=T), in_=s)
+                copy(
+                    out=d[:].rearrange("p (c i t) -> p c t i", i=4, t=T),
+                    in_=wide[n, g][:].rearrange("p t (c i) -> p c t i", i=4),
+                )
 
         def quant_o(n, g):
             oq[n, g] = quant(oil[n, g], "oq%d%d" % (n, g), rot, "oq", 8)
@@ -317,36 +339,43 @@ def tile_multiscaleretention_pb_kernel(
         interleave_w(0, 0)
         interleave_w(0, 1)
         load_w(1, 0)
-        group_stats(0)
-        group_combine(0)
-        normalise(0, 0)
-        normalise(0, 1)
-        group_stats(1)
-        for t in range(2):
-            interleave_w_quarter(0, 1, t)
-        group_combine(1)
-        interleave_w(0, 2)
-        normalise(1, 0)
-        normalise(1, 1)
-        group_stats(2)
-        for t in range(2, 4):
-            interleave_w_quarter(0, 1, t)
+        group_stats(0, 0, 16)
+        group_stats(1, 0, 16)
+        for k in range(4):
+            interleave_w_quarter(0, 1, k)
         load_w(1, 1)
+        group_stats(2, 0, 2)
+        combine_a(0)
+        group_stats(2, 2, 4)
+        combine_b(0)
+        group_stats(2, 4, 6)
+        combine_c(0)
+        group_stats(2, 6, 16)
+        combine_d(0)
+        interleave_w(0, 2)
         load_w(1, 2)
-        group_combine(2)
-        normalise(2, 0)
-        normalise(2, 1)
-        group_stats(3)
-        group_combine(3)
+        for i in range(2):
+            normalise(i, 0)
+            normalise(i, 1)
+        group_stats(3, 0, 16)
         nc.gpsimd.tensor_copy(out=vecs[:], in_=vecs16[:])
         for c in range(NP):
             transpose_x(c, 0)
-            copy_x(c, 0)
-        for c in range(3):
-            quant_w(0, c)
+        combine_a(1)
+        copy_x(0, 0)
+        combine_b(1)
+        copy_x(1, 0)
+        combine_c(1)
+        copy_x(2, 0)
+        copy_x(3, 0)
+        quant_w(0, 0)
+        combine_d(1)
+        quant_w(0, 1)
+        quant_w(0, 2)
         interleave_w(0, 3)
         load_w(1, 3)
-        normalise(3, 0)
+        for i in range(2, 4):
+            normalise(i, 0)
         for c in range(NP):
             transpose_x(c, 1)
             copy_x(c, 1)
@@ -356,15 +385,19 @@ def tile_multiscaleretention_pb_kernel(
             xq[c] = quant(xil[c], "xq%d" % c, keep, "xq%d" % c, 1)
         for k in range(4):
             load_w(2, k)
-        normalise(3, 1)
+        for i in range(2, 4):
+            normalise(i, 1)
         gain(0)
-        interleave_w(1, 2)
 
         for g in range(NP):
+            if g + 1 < NP:
+                for c in range(NP):
+                    if IL_W[g + 1][c] in "TS":
+                        interleave_w(g + 1, c)
             gemm1(g)
             if g + 1 < NP:
                 for c in range(NP):
-                    if IL_W[g + 1][c] == "V":
+                    if IL_W[g + 1][c] in "VU":
                         interleave_w(g + 1, c)
                 for c in range(NP):
                     quant_w(g + 1, c)
@@ -380,9 +413,6 @@ def tile_multiscaleretention_pb_kernel(
                 transpose_norm(g + 1)
                 gain(g + 1)
             if g + 2 < NP:
-                for c in range(NP):
-                    if IL_W[g + 2][c] == "S":
-                        interleave_w(g + 2, c)
                 for i in range(NI):
                     normalise(i, g + 2)
             if g == NP - 2:

@@ -23,8 +23,10 @@ FP8X4 = mybir.dt.float8_e4m3fn_x4
 ALU = mybir.AluOpType
 ACT = mybir.ActivationFunctionType
 
-IL_W = ("SPSV", "VVSV", "VVSV", "VVVV")
-IL_O = "VVVVVVVVVVVVVVVV"
+IL_W = ("SSSV", "VVVV", "VVTV", "VVTV")
+IL_O = "VVVVVVVVVVVVVVVSVSSS"
+X_COPY = ("VS", "VS", "SS", "SS")
+CHUNKS = ((0, 512), (512, 512), (1024, 512), (1536, 256), (1792, 256))
 
 
 def tile_multiscaleretention_pb_kernel(
@@ -46,7 +48,7 @@ def tile_multiscaleretention_pb_kernel(
         def bank(name):
             return psum.tile([P, 512], F32, tag="bank", name=name, bufs=8)
 
-        def il_tile(name, tag="il", bufs=6):
+        def il_tile(name, tag="il", bufs=5):
             return rot.tile([P, T * 512], BF16, tag=tag, name=name, bufs=bufs, align_bytes=64)
 
         at, xs, wraw = [], [], {}
@@ -69,31 +71,44 @@ def tile_multiscaleretention_pb_kernel(
             nc.sync.dma_start(out=a[:], in_=wg4[c][:, :, g * 512 : (g + 1) * 512])
             wraw[g, c] = a
 
-        vecs16 = keep.tile([P, 3, NP, T], BF16, name="vecs16")
-        wsc = keep.tile([P, NP, T], F32, name="wsc")
+        rows16 = rot.tile([P, KP], BF16, tag="nrm", name="rows16", bufs=8, align_bytes=64)
+        rows32 = rot.tile([P, KP], F32, tag="nrm", name="rows32", bufs=8, align_bytes=64)
+        nc.vector.memset(rows16[:], 0.0)
+        nc.vector.memset(rows32[:], 0.0)
         for v, vec in enumerate((bg, gn_w, gn_b)):
-            nc.scalar.dma_start(out=vecs16[:, v, :, :], in_=vec.rearrange("(g p t) -> p g t", p=P, t=T))
-        nc.scalar.dma_start(out=wsc[:], in_=Wo_scale.rearrange("(g p t) o -> p g (t o)", p=P, t=T))
+            nc.scalar.dma_start(out=rows16[v * NP : (v + 1) * NP, :], in_=vec.rearrange("(g c) -> g c", g=NP))
+        nc.scalar.dma_start(out=rows32[0:NP, :], in_=Wo_scale.rearrange("(g c) o -> g (c o)", g=NP))
 
-        for i in range(NI):
+        for i in range(3):
             load_attn(i)
             load_w(0, i)
+        load_attn(3)
         for i in range(NI):
             load_x(i)
+        load_w(0, 3)
 
         warm = keep.tile([P, 1], F32, name="warm")
         nc.vector.memset(warm[:], 0.0)
-        nc.scalar.activation(out=warm[:], in_=warm[:], func=ACT.Silu)
+        nc.scalar.activation(out=warm[:], in_=warm[:], func=ACT.Sqrt)
         ident = keep.tile([P, P], F32, name="ident")
         make_identity(nc, ident[:])
         identb = keep.tile([P, P], BF16, name="identb")
         nc.gpsimd.tensor_copy(out=identb[:], in_=ident[:])
-        mhalf = keep.tile([P, 2, 16], F32, name="mhalf")
-        nc.gpsimd.memset(mhalf[:], -0.5)
-        vecs = keep.tile([P, 3, NP, T], F32, name="vecs")
+        vecs = keep.tile([P, T, 3 * NP], F32, name="vecs")
+        wsc = keep.tile([P, T, NP], F32, name="wsc")
+
+        def spread_vectors():
+            b = psum.tile([P, T, P], BF16, tag="bank", name="bvec", bufs=8)
+            for t in range(T):
+                nc.tensor.transpose(b[:, t, :], rows16[:, t::T], identb[:])
+            nc.scalar.copy(out=vecs[:], in_=b[:, :, 0 : 3 * NP])
+            b = psum.tile([P, T, P], F32, tag="bank", name="bscale", bufs=8)
+            for t in range(T):
+                nc.tensor.transpose(b[:, t, :], rows32[:, t::T], ident[:])
+            nc.scalar.copy(out=wsc[:], in_=b[:, :, 0:NP])
 
         def col(v, g, t):
-            return vecs[:, v, g, t : t + 1]
+            return vecs[:, t, v * NP + g : v * NP + g + 1]
 
         stats = keep.tile([P, NI, 16, 6], F32, name="stats")
         msum = keep.tile([P, NI, 16], F32, name="msum")
@@ -128,7 +143,14 @@ def tile_multiscaleretention_pb_kernel(
             e.scalar_tensor_tensor(
                 out=var[:, k], in0=var[:, k], scalar=1.0 / HD, in1=mdif[:, k], op0=ALU.mult, op1=ALU.add
             )
-            nc.gpsimd.tensor_tensor(out=rstd[:, k], in0=var[:, k], in1=mhalf[:], op=ALU.pow)
+
+        def square_root(b):
+            k = slice(2 * b, 2 * b + 2)
+            nc.scalar.activation(out=var[:, k], in_=var[:, k], func=ACT.Sqrt)
+
+        def reciprocal(b):
+            k = slice(2 * b, 2 * b + 2)
+            nc.vector.reciprocal(out=rstd[:, k], in_=var[:, k])
 
         def combine_d(b):
             k = slice(2 * b, 2 * b + 2)
@@ -176,20 +198,20 @@ def tile_multiscaleretention_pb_kernel(
         def copy_x(c, h):
             if h == 0:
                 xil[c] = il_tile("xil%d" % c)
-            copy = nc.vector.tensor_copy if h == 0 else nc.scalar.copy
+            copy = nc.vector.tensor_copy if X_COPY[c][h] == "V" else nc.scalar.copy
             copy(
                 out=xil[c][:].bitcast(F32)[:, 512 * h : 512 * (h + 1)].rearrange("p (r u) -> p r u", u=2),
                 in_=xbank[c, h][:].rearrange("p (u r) -> p r u", u=2),
             )
 
-        def quant(src, name, codes_pool, tag, bufs):
-            codes = codes_pool.tile([P, 512], U32, tag=tag + "c", name=name + "c", bufs=bufs, align_bytes=64)
-            scales = codes_pool.tile([P, 512], U8, tag=tag + "s", name=name + "s", bufs=bufs, align_bytes=64)
-            nc.vector.quantize_mx(out=codes[:].bitcast(FP8X4), scales=scales[:], in_=src[:])
+        def quant(src, name, codes_pool, tag, bufs, width=512):
+            codes = codes_pool.tile([P, width], U32, tag=tag + "c", name=name + "c", bufs=bufs, align_bytes=64)
+            scales = codes_pool.tile([P, width], U8, tag=tag + "s", name=name + "s", bufs=bufs, align_bytes=64)
+            nc.vector.quantize_mx(out=codes[:].bitcast(FP8X4), scales=scales[:], in_=src[:, 0 : T * width])
             return codes, scales
 
         def tensor_interleave(d, sources, name, eng):
-            for half in range(2):
+            for half in range(len(sources) // 2):
                 b = psum.tile([P, 1024], BF16, tag="bank", name=name + "ab"[half], bufs=8)
                 for k in range(2):
                     nc.tensor.matmul(
@@ -202,7 +224,7 @@ def tile_multiscaleretention_pb_kernel(
 
         def interleave_w(g, c):
             eng = IL_W[g][c]
-            d = il_tile("wil%d%d" % (g, c), "ils", 2) if eng in "ST" else il_tile("wil%d%d" % (g, c))
+            d = il_tile("wil%d%d" % (g, c), "ils", 3) if eng in "ST" else il_tile("wil%d%d" % (g, c))
             wil[g, c] = d
             o = d[:].rearrange("p (t m j) -> p m j t", t=T, j=T)
             s = wraw[g, c][:].rearrange("p j (m t) -> p m j t", t=T)
@@ -280,49 +302,52 @@ def tile_multiscaleretention_pb_kernel(
             wob[h, g] = b
 
         def widen(n, g):
-            w = rot.tile([P, T, 512], BF16, tag="wide", name="wide%d%d" % (n, g), bufs=4, align_bytes=64)
+            col, width = CHUNKS[n]
+            w = rot.tile([P, T, width], BF16, tag="wide", name="wide%d%d" % (n, g), bufs=4, align_bytes=64)
             wide[n, g] = w
-            lo = (n % 2) * 512
+            lo = col % 1024
             for t in range(T):
                 nc.scalar.activation(
                     out=w[:, t, :],
-                    in_=wob[n // 2, g][:, t, lo : lo + 512].bitcast(FP8),
+                    in_=wob[col // 1024, g][:, t, lo : lo + width].bitcast(FP8),
                     func=ACT.Copy,
-                    scale=wsc[:, g, t : t + 1],
+                    scale=wsc[:, t, g : g + 1],
                 )
 
         def interleave_o(n, g):
+            width = CHUNKS[n][1]
             eng = IL_O[4 * n + g]
-            d = il_tile("oil%d%d" % (n, g), "ils", 2) if eng in "ST" else il_tile("oil%d%d" % (n, g))
+            d = il_tile("oil%d%d" % (n, g), "ils", 3) if eng in "ST" else il_tile("oil%d%d" % (n, g))
             oil[n, g] = d
             s = wide[n, g][:].rearrange("p t n -> p n t")
             if eng in "TU":
-                tensor_interleave(d, [s[:, k * P : (k + 1) * P] for k in range(4)], "po%d%d" % (n, g), eng)
+                tensor_interleave(d, [s[:, k * P : (k + 1) * P] for k in range(width // P)], "po%d%d" % (n, g), eng)
             else:
                 copy = nc.scalar.copy if eng == "S" else nc.vector.tensor_copy
                 copy(
-                    out=d[:].rearrange("p (c i t) -> p c t i", i=4, t=T),
+                    out=d[:, 0 : T * width].rearrange("p (c i t) -> p c t i", i=4, t=T),
                     in_=wide[n, g][:].rearrange("p t (c i) -> p c t i", i=4),
                 )
 
         def quant_o(n, g):
-            oq[n, g] = quant(oil[n, g], "oq%d%d" % (n, g), rot, "oq", 8)
+            oq[n, g] = quant(oil[n, g], "oq%d%d" % (n, g), rot, "oq", 8, CHUNKS[n][1])
 
         acc2 = {}
 
-        def gemm2(n):
-            for i in range(NI):
-                acc2[n, i] = bank("out%d%d" % (n, i))
-            for g in range(NP):
+        def gemm2(n, gs):
+            width = CHUNKS[n][1]
+            for g in gs:
                 hc, hs = hq[g]
                 codes, scales = oq[n, g]
                 for i in range(NI):
+                    if g == 0:
+                        acc2[n, i] = bank("out%d%d" % (n, i))
                     nc.tensor.matmul_mx(
-                        out=acc2[n, i][:],
+                        out=acc2[n, i][:, 0:width],
                         lhsT=hc[:, i * P : (i + 1) * P].bitcast(FP8X4),
                         lhsT_scale=hs[:, i * P : (i + 1) * P],
-                        rhs=codes[:].bitcast(FP8X4),
-                        rhs_scale=scales[:],
+                        rhs=codes[:, 0:width].bitcast(FP8X4),
+                        rhs_scale=scales[:, 0:width],
                         start=(g == 0),
                         stop=(g == NP - 1),
                     )
@@ -330,74 +355,93 @@ def tile_multiscaleretention_pb_kernel(
         bo_sb = keep.tile([P, E], BF16, name="bo_sb")
 
         def store(n):
+            col, width = CHUNKS[n]
+            cols = slice(col, col + width)
             for i in range(NI):
-                o = rot.tile([P, 512], F32, tag="o", name="o%d%d" % (n, i), bufs=4, align_bytes=64)
-                cols = slice(n * 512, (n + 1) * 512)
-                nc.vector.tensor_tensor(out=o[:], in0=acc2[n, i][:], in1=bo_sb[:, cols], op=ALU.add)
+                o = rot.tile([P, width], F32, tag="o", name="o%d%d" % (n, i), bufs=4, align_bytes=64)
+                nc.vector.tensor_tensor(out=o[:], in0=acc2[n, i][:, 0:width], in1=bo_sb[:, cols], op=ALU.add)
                 nc.sync.dma_start(out=out2[i * P : (i + 1) * P, cols], in_=o[:])
 
-        interleave_w(0, 0)
-        interleave_w(0, 1)
-        load_w(1, 0)
+        def warm_up(src, count, name):
+            b = bank(name)
+            for k in range(count):
+                nc.tensor.matmul(b[:], lhsT=identb[:], rhs=src[:, 0:512], start=True, stop=True)
+
         group_stats(0, 0, 16)
-        group_stats(1, 0, 16)
-        for k in range(4):
-            interleave_w_quarter(0, 1, k)
+        spread_vectors()
+        interleave_w(0, 0)
+        load_w(1, 0)
+        interleave_w(0, 1)
         load_w(1, 1)
+        group_stats(1, 0, 16)
         group_stats(2, 0, 2)
         combine_a(0)
         group_stats(2, 2, 4)
         combine_b(0)
         group_stats(2, 4, 6)
         combine_c(0)
-        group_stats(2, 6, 16)
-        combine_d(0)
+        square_root(0)
         interleave_w(0, 2)
         load_w(1, 2)
+        group_stats(2, 6, 10)
+        reciprocal(0)
+        group_stats(2, 10, 12)
+        combine_d(0)
+        group_stats(2, 12, 16)
         for i in range(2):
             normalise(i, 0)
             normalise(i, 1)
         group_stats(3, 0, 16)
-        nc.gpsimd.tensor_copy(out=vecs[:], in_=vecs16[:])
+        warm_up(at[3], 4, "warm0")
         for c in range(NP):
             transpose_x(c, 0)
+            if c % 2 == 1:
+                warm_up(xs[0], 2, "warm1%d" % c)
         combine_a(1)
         copy_x(0, 0)
         combine_b(1)
         copy_x(1, 0)
         combine_c(1)
+        square_root(1)
+        nc.scalar.activation(out=warm[:], in_=warm[:], func=ACT.Silu)
         copy_x(2, 0)
         copy_x(3, 0)
         quant_w(0, 0)
-        combine_d(1)
+        reciprocal(1)
         quant_w(0, 1)
+        combine_d(1)
         quant_w(0, 2)
-        interleave_w(0, 3)
-        load_w(1, 3)
-        for i in range(2, 4):
-            normalise(i, 0)
         for c in range(NP):
             transpose_x(c, 1)
+            if c % 2 == 1:
+                warm_up(xs[2], 2, "warm2%d" % c)
             copy_x(c, 1)
-        transpose_norm(0)
-        quant_w(0, 3)
+        for i in range(2, 4):
+            normalise(i, 0)
+        interleave_w(0, 3)
+        load_w(1, 3)
         for c in range(NP):
             xq[c] = quant(xil[c], "xq%d" % c, keep, "xq%d" % c, 1)
+        quant_w(0, 3)
+        for c in range(NP):
+            if IL_W[1][c] in "TS":
+                interleave_w(1, c)
+        transpose_norm(0)
         for k in range(4):
             load_w(2, k)
+        gain(0)
         for i in range(2, 4):
             normalise(i, 1)
-        gain(0)
 
         for g in range(NP):
-            if g + 1 < NP:
+            if 0 < g < NP - 1:
                 for c in range(NP):
                     if IL_W[g + 1][c] in "TS":
                         interleave_w(g + 1, c)
             gemm1(g)
             if g + 1 < NP:
                 for c in range(NP):
-                    if IL_W[g + 1][c] in "VU":
+                    if IL_W[g + 1][c] == "V" and (g + 1, c) not in wil:
                         interleave_w(g + 1, c)
                 for c in range(NP):
                     quant_w(g + 1, c)
@@ -408,6 +452,9 @@ def tile_multiscaleretention_pb_kernel(
                     for k in range(NP):
                         load_wo(0, k)
                     nc.sync.dma_start(out=bo_sb[:], in_=bo.partition_broadcast(P))
+            if g == NP - 1:
+                widen(0, 0)
+                interleave_o(0, 0)
             silu(g)
             if g + 1 < NP:
                 transpose_norm(g + 1)
@@ -415,16 +462,15 @@ def tile_multiscaleretention_pb_kernel(
             if g + 2 < NP:
                 for i in range(NI):
                     normalise(i, g + 2)
-            if g == NP - 2:
-                widen(0, 0)
-                widen(0, 1)
-            if g == NP - 1:
-                interleave_o(0, 0)
-                interleave_o(0, 1)
+            if g + 2 < NP:
+                interleave_w(g + 2, 0)
             product(g)
+            if g == NP - 1:
+                widen(0, 1)
+                interleave_o(0, 1)
             quant_h(g)
 
-        units = [(n, g) for n in range(4) for g in range(NP)]
+        units = [(n, g) for n in range(len(CHUNKS)) for g in range(NP)]
         for k, (n, g) in enumerate(units):
             if k + 2 < len(units):
                 widen(*units[k + 2])
@@ -432,8 +478,7 @@ def tile_multiscaleretention_pb_kernel(
                     load_wo(1, k - 2)
                 interleave_o(*units[k + 2])
             quant_o(n, g)
-            if g == NP - 1:
-                gemm2(n)
-            if g == 1 and n > 0:
+            if g == 0 and n > 0:
                 store(n - 1)
-        store(3)
+            gemm2(n, (g,))
+        store(len(CHUNKS) - 1)

from contextlib import ExitStack

import concourse.mybir as mybir
from concourse.masks import make_identity

TOK, E = 512, 2048
HD = 128
EPS = 1e-5
FLOPS = 2 * (2 * TOK * E * E)

P = 128
T = 4
KP = P * T
NP = E // KP
NI = TOK // P

F32 = mybir.dt.float32
BF16 = mybir.dt.bfloat16
U32 = mybir.dt.uint32
U8 = mybir.dt.uint8
FP8 = mybir.dt.float8_e4m3fn
FP8X4 = mybir.dt.float8_e4m3fn_x4
ALU = mybir.AluOpType
ACT = mybir.ActivationFunctionType

IL_W = ("SSSV", "VVVV", "VVTV", "VVTV")
IL_O = "VVVVVVVVVVVVVVVSVSSS"
X_COPY = ("VS", "VS", "SS", "SS")
CHUNKS = ((0, 512), (512, 512), (1024, 512), (1536, 256), (1792, 256))


def tile_multiscaleretention_pb_kernel(
    tc, x, attn, Wg, bg, gn_w, gn_b, Wo_bytes, Wo_scale, bo, out
):
    nc = tc.nc
    x2 = x.rearrange("o s e -> (o s) e")
    a2 = attn.rearrange("o s e -> (o s) e")
    out2 = out.rearrange("o s e -> (o s) e")
    wg4 = Wg.rearrange("(c p j) n -> c p j n", p=P, j=T)
    wo4 = Wo_bytes.rearrange("(g p t) n -> g p t n", p=P, t=T)

    with ExitStack() as ctx:
        keep = ctx.enter_context(tc.tile_pool(name="keep", bufs=1))
        rot = ctx.enter_context(tc.tile_pool(name="rot", bufs=2))
        psum = ctx.enter_context(tc.psum_pool(name="psum", bufs=8))
        ctx.enter_context(tc.manual_schedule())

        def bank(name):
            return psum.tile([P, 512], F32, tag="bank", name=name, bufs=8)

        def il_tile(name, tag="il", bufs=5):
            return rot.tile([P, T * 512], BF16, tag=tag, name=name, bufs=bufs, align_bytes=64)

        at, xs, wraw = [], [], {}

        def load_attn(i):
            a = keep.tile([P, E], BF16, name="at%d" % i, align_bytes=64)
            pieces = 2 if i == 0 else 1
            for k in range(pieces):
                cols = slice(k * E // pieces, (k + 1) * E // pieces)
                nc.sync.dma_start(out=a[:, cols], in_=a2[i * P : (i + 1) * P, cols])
            at.append(a)

        def load_x(i):
            a = rot.tile([P, E], BF16, tag="in4k", name="xs%d" % i, bufs=8, align_bytes=64)
            nc.sync.dma_start(out=a[:], in_=x2[i * P : (i + 1) * P, :])
            xs.append(a)

        def load_w(g, c):
            a = rot.tile([P, T, 512], BF16, tag="in4k", name="w%d%d" % (g, c), bufs=8, align_bytes=64)
            nc.sync.dma_start(out=a[:], in_=wg4[c][:, :, g * 512 : (g + 1) * 512])
            wraw[g, c] = a

        rows16 = rot.tile([P, KP], BF16, tag="nrm", name="rows16", bufs=8, align_bytes=64)
        rows32 = rot.tile([P, KP], F32, tag="nrm", name="rows32", bufs=8, align_bytes=64)
        nc.vector.memset(rows16[:], 0.0)
        nc.vector.memset(rows32[:], 0.0)
        for v, vec in enumerate((bg, gn_w, gn_b)):
            nc.scalar.dma_start(out=rows16[v * NP : (v + 1) * NP, :], in_=vec.rearrange("(g c) -> g c", g=NP))
        nc.scalar.dma_start(out=rows32[0:NP, :], in_=Wo_scale.rearrange("(g c) o -> g (c o)", g=NP))

        for i in range(3):
            load_attn(i)
            load_w(0, i)
        load_attn(3)
        for i in range(NI):
            load_x(i)
        load_w(0, 3)

        warm = keep.tile([P, 1], F32, name="warm")
        nc.vector.memset(warm[:], 0.0)
        nc.scalar.activation(out=warm[:], in_=warm[:], func=ACT.Sqrt)
        ident = keep.tile([P, P], F32, name="ident")
        make_identity(nc, ident[:])
        identb = keep.tile([P, P], BF16, name="identb")
        nc.gpsimd.tensor_copy(out=identb[:], in_=ident[:])
        vecs = keep.tile([P, T, 3 * NP], F32, name="vecs")
        wsc = keep.tile([P, T, NP], F32, name="wsc")

        def spread_vectors():
            b = psum.tile([P, T, P], BF16, tag="bank", name="bvec", bufs=8)
            for t in range(T):
                nc.tensor.transpose(b[:, t, :], rows16[:, t::T], identb[:])
            nc.scalar.copy(out=vecs[:], in_=b[:, :, 0 : 3 * NP])
            b = psum.tile([P, T, P], F32, tag="bank", name="bscale", bufs=8)
            for t in range(T):
                nc.tensor.transpose(b[:, t, :], rows32[:, t::T], ident[:])
            nc.scalar.copy(out=wsc[:], in_=b[:, :, 0:NP])

        def col(v, g, t):
            return vecs[:, t, v * NP + g : v * NP + g + 1]

        stats = keep.tile([P, NI, 16, 6], F32, name="stats")
        msum = keep.tile([P, NI, 16], F32, name="msum")
        mdif = keep.tile([P, NI, 16], F32, name="mdif")
        var = keep.tile([P, NI, 16], F32, name="var")
        rstd = keep.tile([P, NI, 16], F32, name="rstd")
        nbias = keep.tile([P, NI, 16], F32, name="nbias")

        def group_stats(i, lo, hi):
            for q in range(lo, hi):
                nc.vector.bn_stats(out=stats[:, i, q, :], in_=at[i][:, q * HD : (q + 1) * HD])

        def combine_a(b):
            e, s = nc.vector, stats[:, 2 * b : 2 * b + 2]
            k = slice(2 * b, 2 * b + 2)
            e.tensor_tensor(out=mdif[:, k], in0=s[:, :, :, 1], in1=s[:, :, :, 4], op=ALU.subtract)
            e.scalar_tensor_tensor(
                out=var[:, k], in0=s[:, :, :, 2], scalar=HD * EPS, in1=s[:, :, :, 5], op0=ALU.add, op1=ALU.add
            )
            e.tensor_tensor(out=msum[:, k], in0=s[:, :, :, 1], in1=s[:, :, :, 4], op=ALU.add)

        def combine_b(b):
            e = nc.vector
            k = slice(2 * b, 2 * b + 2)
            e.scalar_tensor_tensor(
                out=mdif[:, k], in0=mdif[:, k], scalar=0.25, in1=mdif[:, k], op0=ALU.mult, op1=ALU.mult
            )

        def combine_c(b):
            e = nc.vector
            k = slice(2 * b, 2 * b + 2)
            e.scalar_tensor_tensor(
                out=var[:, k], in0=var[:, k], scalar=1.0 / HD, in1=mdif[:, k], op0=ALU.mult, op1=ALU.add
            )

        def square_root(b):
            k = slice(2 * b, 2 * b + 2)
            nc.scalar.activation(out=var[:, k], in_=var[:, k], func=ACT.Sqrt)

        def reciprocal(b):
            k = slice(2 * b, 2 * b + 2)
            nc.vector.reciprocal(out=rstd[:, k], in_=var[:, k])

        def combine_d(b):
            k = slice(2 * b, 2 * b + 2)
            nc.vector.scalar_tensor_tensor(
                out=nbias[:, k], in0=msum[:, k], scalar=-0.5, in1=rstd[:, k], op0=ALU.mult, op1=ALU.mult
            )

        nrm = {}

        def normalise(i, g):
            n = rot.tile([P, T, P], F32, tag="nrm", name="nrm%d%d" % (i, g), bufs=8, align_bytes=64)
            nrm[i, g] = n
            for u in range(4):
                q = 4 * g + u
                nc.scalar.activation(
                    out=n[:, :, 32 * u : 32 * (u + 1)].rearrange("p t m -> p m t"),
                    in_=at[i][:, q * HD : (q + 1) * HD].rearrange("p (m t) -> p m t", t=T),
                    func=ACT.Identity,
                    scale=rstd[:, i, q : q + 1],
                    bias=nbias[:, i, q : q + 1],
                )

        nbank = {}

        def transpose_norm(g):
            for t in range(T):
                b = bank("nT%d%d" % (g, t))
                nbank[g, t] = b
                for i in range(NI):
                    nc.tensor.transpose(b[:, i * P : (i + 1) * P], nrm[i, g][:, t, :], ident[:])

        xbank, xil, xq, xqs = {}, {}, {}, {}

        def transpose_x(c, h):
            b = bank("xT%d%d" % (c, h))
            xbank[c, h] = b
            bv = b[:].rearrange("p (u r) -> p u r", u=2)
            for i in range(2):
                words = xs[2 * h + i][:].bitcast(F32)
                for u in range(2):
                    nc.tensor.transpose(
                        bv[:, u, i * P : (i + 1) * P], words[:, 256 * c + u : 256 * (c + 1) : 2], ident[:]
                    )

        def copy_x(c, h):
            if h == 0:
                xil[c] = il_tile("xil%d" % c)
            copy = nc.vector.tensor_copy if X_COPY[c][h] == "V" else nc.scalar.copy
            copy(
                out=xil[c][:].bitcast(F32)[:, 512 * h : 512 * (h + 1)].rearrange("p (r u) -> p r u", u=2),
                in_=xbank[c, h][:].rearrange("p (u r) -> p r u", u=2),
            )

        def quant(src, name, codes_pool, tag, bufs, width=512):
            codes = codes_pool.tile([P, width], U32, tag=tag + "c", name=name + "c", bufs=bufs, align_bytes=64)
            scales = codes_pool.tile([P, width], U8, tag=tag + "s", name=name + "s", bufs=bufs, align_bytes=64)
            nc.vector.quantize_mx(out=codes[:].bitcast(FP8X4), scales=scales[:], in_=src[:, 0 : T * width])
            return codes, scales

        def tensor_interleave(d, sources, name, eng):
            for half in range(len(sources) // 2):
                b = psum.tile([P, 1024], BF16, tag="bank", name=name + "ab"[half], bufs=8)
                for k in range(2):
                    nc.tensor.matmul(
                        b[:, 512 * k : 512 * (k + 1)], lhsT=identb[:], rhs=sources[2 * half + k], start=True, stop=True
                    )
                copy = nc.scalar.copy if eng == "T" else nc.vector.tensor_copy
                copy(out=d[:, 1024 * half : 1024 * (half + 1)], in_=b[:])

        wil, wq = {}, {}

        def interleave_w(g, c):
            eng = IL_W[g][c]
            d = il_tile("wil%d%d" % (g, c), "ils", 3) if eng in "ST" else il_tile("wil%d%d" % (g, c))
            wil[g, c] = d
            o = d[:].rearrange("p (t m j) -> p m j t", t=T, j=T)
            s = wraw[g, c][:].rearrange("p j (m t) -> p m j t", t=T)
            if eng in "TU":
                s = wraw[g, c][:].rearrange("p j (m t) -> p t m j", t=T)
                tensor_interleave(d, [s[:, t] for t in range(T)], "pw%d%d" % (g, c), eng)
            elif eng == "V":
                nc.vector.tensor_copy(out=o, in_=s)
            elif eng == "S":
                nc.scalar.copy(out=o, in_=s)

        def interleave_w_quarter(g, c, k):
            o = wil[g, c][:].rearrange("p (t m j) -> p m t j", t=T, j=T)
            s = wraw[g, c][:].rearrange("p j (m t) -> p m t j", t=T)
            m = slice(32 * k, 32 * (k + 1))
            nc.gpsimd.tensor_scalar(
                out=o[:, m, :, :], in0=s[:, m, :, :], scalar1=1.0, scalar2=0.0, op0=ALU.mult, op1=ALU.add
            )

        def quant_w(g, c):
            wq[g, c] = quant(wil[g, c], "wq%d%d" % (g, c), rot, "wq", 8)

        acc, fT, gate, hq = {}, {}, {}, {}

        def gemm1(g):
            for t in range(T):
                b = bank("acc%d%d" % (g, t))
                acc[g, t] = b
                for c in range(NP):
                    codes, scales = wq[g, c]
                    nc.tensor.matmul_mx(
                        out=b[:],
                        lhsT=codes[:, t * P : (t + 1) * P].bitcast(FP8X4),
                        lhsT_scale=scales[:, t * P : (t + 1) * P],
                        rhs=xq[c][0][:].bitcast(FP8X4),
                        rhs_scale=xq[c][1][:],
                        start=(c == 0),
                        stop=(c == NP - 1),
                    )

        def gain(g):
            f = rot.tile([P, T, TOK], F32, tag="f", name="f%d" % g, bufs=2, align_bytes=64)
            fT[g] = f
            for t in range(T):
                nc.scalar.activation(
                    out=f[:, t, :], in_=nbank[g, t][:], func=ACT.Identity, scale=col(1, g, t), bias=col(2, g, t)
                )

        def silu(g):
            f = rot.tile([P, T, TOK], F32, tag="gate", name="gate%d" % g, bufs=2, align_bytes=64)
            gate[g] = f
            for t in range(T):
                nc.scalar.activation(out=f[:, t, :], in_=acc[g, t][:], func=ACT.Silu, bias=col(0, g, t))

        hil = {}

        def product(g):
            d = il_tile("hil%d" % g)
            hil[g] = d
            nc.vector.tensor_tensor(
                out=d[:].rearrange("p (c i t) -> p c t i", i=4, t=T),
                in0=fT[g][:].rearrange("p t (c i) -> p c t i", i=4),
                in1=gate[g][:].rearrange("p t (c i) -> p c t i", i=4),
                op=ALU.mult,
            )

        def quant_h(g):
            hq[g] = quant(hil[g], "hq%d" % g, keep, "hq%d" % g, 1)

        wob, wide, oil, oq = {}, {}, {}, {}

        def load_wo(h, g):
            b = rot.tile([P, T, 1024], U8, tag="wob", name="wob%d%d" % (h, g), bufs=4, align_bytes=64)
            nc.sync.dma_start(out=b[:], in_=wo4[g][:, :, h * 1024 : (h + 1) * 1024])
            wob[h, g] = b

        def widen(n, g):
            col, width = CHUNKS[n]
            w = rot.tile([P, T, width], BF16, tag="wide", name="wide%d%d" % (n, g), bufs=4, align_bytes=64)
            wide[n, g] = w
            lo = col % 1024
            for t in range(T):
                nc.scalar.activation(
                    out=w[:, t, :],
                    in_=wob[col // 1024, g][:, t, lo : lo + width].bitcast(FP8),
                    func=ACT.Copy,
                    scale=wsc[:, t, g : g + 1],
                )

        def interleave_o(n, g):
            width = CHUNKS[n][1]
            eng = IL_O[4 * n + g]
            d = il_tile("oil%d%d" % (n, g), "ils", 3) if eng in "ST" else il_tile("oil%d%d" % (n, g))
            oil[n, g] = d
            s = wide[n, g][:].rearrange("p t n -> p n t")
            if eng in "TU":
                tensor_interleave(d, [s[:, k * P : (k + 1) * P] for k in range(width // P)], "po%d%d" % (n, g), eng)
            else:
                copy = nc.scalar.copy if eng == "S" else nc.vector.tensor_copy
                copy(
                    out=d[:, 0 : T * width].rearrange("p (c i t) -> p c t i", i=4, t=T),
                    in_=wide[n, g][:].rearrange("p t (c i) -> p c t i", i=4),
                )

        def quant_o(n, g):
            oq[n, g] = quant(oil[n, g], "oq%d%d" % (n, g), rot, "oq", 8, CHUNKS[n][1])

        acc2 = {}

        def gemm2(n, gs):
            width = CHUNKS[n][1]
            for g in gs:
                hc, hs = hq[g]
                codes, scales = oq[n, g]
                for i in range(NI):
                    if g == 0:
                        acc2[n, i] = bank("out%d%d" % (n, i))
                    nc.tensor.matmul_mx(
                        out=acc2[n, i][:, 0:width],
                        lhsT=hc[:, i * P : (i + 1) * P].bitcast(FP8X4),
                        lhsT_scale=hs[:, i * P : (i + 1) * P],
                        rhs=codes[:, 0:width].bitcast(FP8X4),
                        rhs_scale=scales[:, 0:width],
                        start=(g == 0),
                        stop=(g == NP - 1),
                    )

        bo_sb = keep.tile([P, E], BF16, name="bo_sb")

        def store(n):
            col, width = CHUNKS[n]
            cols = slice(col, col + width)
            for i in range(NI):
                o = rot.tile([P, width], F32, tag="o", name="o%d%d" % (n, i), bufs=4, align_bytes=64)
                nc.vector.tensor_tensor(out=o[:], in0=acc2[n, i][:, 0:width], in1=bo_sb[:, cols], op=ALU.add)
                nc.sync.dma_start(out=out2[i * P : (i + 1) * P, cols], in_=o[:])

        def warm_up(src, count, name):
            b = bank(name)
            for k in range(count):
                nc.tensor.matmul(b[:], lhsT=identb[:], rhs=src[:, 0:512], start=True, stop=True)

        group_stats(0, 0, 16)
        spread_vectors()
        interleave_w(0, 0)
        load_w(1, 0)
        interleave_w(0, 1)
        load_w(1, 1)
        group_stats(1, 0, 16)
        group_stats(2, 0, 2)
        combine_a(0)
        group_stats(2, 2, 4)
        combine_b(0)
        group_stats(2, 4, 6)
        combine_c(0)
        square_root(0)
        interleave_w(0, 2)
        load_w(1, 2)
        group_stats(2, 6, 10)
        reciprocal(0)
        group_stats(2, 10, 12)
        combine_d(0)
        group_stats(2, 12, 16)
        for i in range(2):
            normalise(i, 0)
            normalise(i, 1)
        group_stats(3, 0, 16)
        warm_up(at[3], 4, "warm0")
        for c in range(NP):
            transpose_x(c, 0)
            if c % 2 == 1:
                warm_up(xs[0], 2, "warm1%d" % c)
        combine_a(1)
        copy_x(0, 0)
        combine_b(1)
        copy_x(1, 0)
        combine_c(1)
        square_root(1)
        nc.scalar.activation(out=warm[:], in_=warm[:], func=ACT.Silu)
        copy_x(2, 0)
        copy_x(3, 0)
        quant_w(0, 0)
        reciprocal(1)
        quant_w(0, 1)
        combine_d(1)
        quant_w(0, 2)
        for c in range(NP):
            transpose_x(c, 1)
            if c % 2 == 1:
                warm_up(xs[2], 2, "warm2%d" % c)
            copy_x(c, 1)
        for i in range(2, 4):
            normalise(i, 0)
        interleave_w(0, 3)
        load_w(1, 3)
        for c in range(NP):
            xq[c] = quant(xil[c], "xq%d" % c, keep, "xq%d" % c, 1)
        quant_w(0, 3)
        for c in range(NP):
            if IL_W[1][c] in "TS":
                interleave_w(1, c)
        transpose_norm(0)
        for k in range(4):
            load_w(2, k)
        gain(0)
        for i in range(2, 4):
            normalise(i, 1)

        for g in range(NP):
            if 0 < g < NP - 1:
                for c in range(NP):
                    if IL_W[g + 1][c] in "TS":
                        interleave_w(g + 1, c)
            gemm1(g)
            if g + 1 < NP:
                for c in range(NP):
                    if IL_W[g + 1][c] == "V" and (g + 1, c) not in wil:
                        interleave_w(g + 1, c)
                for c in range(NP):
                    quant_w(g + 1, c)
                if g < 1:
                    for k in range(4):
                        load_w(3, k)
                if g == 1:
                    for k in range(NP):
                        load_wo(0, k)
                    nc.sync.dma_start(out=bo_sb[:], in_=bo.partition_broadcast(P))
            if g == NP - 1:
                widen(0, 0)
                interleave_o(0, 0)
            silu(g)
            if g + 1 < NP:
                transpose_norm(g + 1)
                gain(g + 1)
            if g + 2 < NP:
                for i in range(NI):
                    normalise(i, g + 2)
            if g + 2 < NP:
                interleave_w(g + 2, 0)
            product(g)
            if g == NP - 1:
                widen(0, 1)
                interleave_o(0, 1)
            quant_h(g)

        units = [(n, g) for n in range(len(CHUNKS)) for g in range(NP)]
        for k, (n, g) in enumerate(units):
            if k + 2 < len(units):
                widen(*units[k + 2])
                if 4 <= k + 2 < 8:
                    load_wo(1, k - 2)
                interleave_o(*units[k + 2])
            quant_o(n, g)
            if g == 0 and n > 0:
                store(n - 1)
            gemm2(n, (g,))
        store(len(CHUNKS) - 1)
